import numpy as np
import ml_dtypes


def mxq(x, axis, fmt="e4m3"):
    dtype, down = {"e4m3": (ml_dtypes.float8_e4m3fn, 7), "e5m2": (ml_dtypes.float8_e5m2, 14)}[fmt]
    v = np.moveaxis(np.asarray(x, np.float32).astype(ml_dtypes.bfloat16).astype(np.float64), axis, -1)
    blocks = v.reshape(v.shape[:-1] + (-1, 32))
    amax = np.abs(blocks).max(-1, keepdims=True)
    byte = np.maximum(np.where(amax > 0, np.frexp(amax)[1] - 1 + 127, 0) - down, 1)
    scale = np.exp2(byte - 127.0)
    codes = (blocks / scale).astype(np.float32).astype(dtype).astype(np.float64)
    return np.moveaxis((codes * scale).reshape(v.shape), -1, axis)


WIDE = False


def mx_kscale(k):
    if not WIDE:
        return np.ones(k)
    levels = np.array([10, -10, 5, -5, 0])
    a = np.random.permutation(np.resize(levels, k // 512 * 4)).reshape(k // 512, 4)
    idx = np.arange(k)
    return np.exp2(a[idx // 512, idx % 128 // 32])


BF16 = ml_dtypes.bfloat16


def bf(x):
    return np.asarray(x, np.float32).astype(BF16)


def f64(x):
    return np.asarray(x).astype(np.float64)


E2M1 = np.array([0.0, 0.5, 1.0, 1.5, 2.0, 3.0, 4.0, 6.0, -0.0, -0.5, -1.0, -1.5, -2.0, -3.0, -4.0, -6.0])


def pack_weight(w, fmt):
    k, n = w.shape
    w = f64(bf(w)).reshape(k // 32, 32, n)
    amax = np.abs(w).max(1)
    if fmt == "e4m3":
        byte = np.frexp(amax)[1] - 1 + 127 - 7
    else:
        mant, ex = np.frexp(amax / 6.0)
        byte = np.where(mant > 0.5, ex, ex - 1) + 127
    byte = np.clip(np.where(amax > 0, byte, 1), 1, 254)
    scaled = (w * np.exp2(127.0 - byte)[:, None, :]).reshape(k, n).astype(np.float32)
    by_word = np.ascontiguousarray(scaled.reshape(k // 512, 128, 4, n).transpose(0, 1, 3, 2))
    if fmt == "e4m3":
        words = by_word.astype(ml_dtypes.float8_e4m3fn).view(np.uint8)
    else:
        c = by_word.astype(ml_dtypes.float4_e2m1fn).view(np.uint8) & 0xF
        words = c[..., 0::2] | (c[..., 1::2] << 4)
    return np.ascontiguousarray(words), np.ascontiguousarray(byte.astype(np.uint8).reshape(k // 512, 16, n))


def unpack_weight(words, scales, fmt):
    g, p, n, _ = words.shape
    if fmt == "e4m3":
        vals = np.ascontiguousarray(words).view(ml_dtypes.float8_e4m3fn).astype(np.float64)
    else:
        nib = np.empty((g, p, n, 4), np.uint8)
        nib[..., 0::2] = words & 0xF
        nib[..., 1::2] = words >> 4
        vals = E2M1[nib]
    vals = vals * np.repeat(np.exp2(scales.astype(np.float64) - 127.0), 8, axis=1)[..., None]
    return vals.transpose(0, 1, 3, 2).reshape(g * 512, n)


B, C, K, L, R = 4, 64, 512, 16, 128
FMT = "e4m3"


def transition():
    g = np.exp(2.5 * np.random.standard_normal((K, K)))
    return g / g.sum(1, keepdims=True)


def setup_inputs():
    s = mx_kscale(K)
    x = np.random.standard_normal((B, C, K, L)) * 2.0 * s[None, None, :, None]
    words0, scales0 = pack_weight((transition() * s[:, None] / s[None, :]).T, FMT)
    words1, scales1 = pack_weight((transition() * s[:, None] / s[None, :]).T, FMT)
    return {'x': bf(x.reshape(B, C, K * L)),
            'support0_words': words0, 'support0_scales': scales0,
            'support1_words': words1, 'support1_scales': scales1}


def two_hops(xq, aq):
    x1 = xq @ aq
    x2 = mxq(x1, 2, 'e4m3') @ aq
    return x1, x2


def reference(x, support0_words, support0_scales, support1_words, support1_scales):
    xr = f64(x).reshape(B, C, K, L).transpose(0, 3, 1, 2).reshape(B * L, C, K)
    xq = mxq(xr, 2, 'e4m3')
    f1, f2 = two_hops(xq, unpack_weight(support0_words, support0_scales, FMT))
    g1, g2 = two_hops(xq, unpack_weight(support1_words, support1_scales, FMT))
    return f1, f2, g1, g2

@@ -1,0 +1,255 @@
+from contextlib import ExitStack
+
+import concourse.mybir as mybir
+from concourse.masks import make_identity
+
+F32 = mybir.dt.float32
+BF16 = mybir.dt.bfloat16
+I32 = mybir.dt.int32
+U32 = mybir.dt.uint32
+U8 = mybir.dt.uint8
+FP8X4 = mybir.dt.float8_e4m3fn_x4
+
+P = 128
+PACK = 4
+BATCH, CHANNELS, NODES, STEPS = 4, 64, 512, 16
+TILES = 4
+CQ = CHANNELS // TILES
+LL = P // CQ
+UNITS = 16
+X_BANKS = 16
+X_WORDS = NODES * STEPS // 2
+
+TRANSPOSE_LAG = 1
+QUANTISE_LAG = 2
+HOP2_LAG = 3
+X_LEAD = 5
+
+FLOPS = 4 * 2 * BATCH * STEPS * CHANNELS * NODES * NODES
+
+
+def tile_adaptivegcn_pb_t_kernel(
+    tc,
+    x,
+    support0_words,
+    support0_scales,
+    support1_words,
+    support1_scales,
+    out_0,
+    out_1,
+    out_2,
+    out_3,
+):
+    nc = tc.nc
+    words_in = (support0_words, support1_words)
+    scales_in = (support0_scales, support1_scales)
+
+    def by_group(out):
+        return out.rearrange(
+            "(b lh ll) (cq i) w -> b lh cq ll (i w)", b=BATCH, lh=2, ll=LL, cq=CQ, i=TILES
+        )
+
+    hop1_out = (by_group(out_0), by_group(out_2))
+    hop2_out = (by_group(out_1), by_group(out_3))
+
+    with ExitStack() as stack:
+        keep = stack.enter_context(tc.tile_pool(name="keep", bufs=1))
+        stage = stack.enter_context(tc.tile_pool(name="stage", bufs=2))
+        rows_pool = stack.enter_context(tc.tile_pool(name="rows", bufs=4))
+        acc_pool = stack.enter_context(tc.psum_pool(name="acc", bufs=5))
+        flip_pool = stack.enter_context(tc.psum_pool(name="flip", bufs=3))
+        stack.enter_context(tc.manual_schedule())
+
+        x_rows = x.rearrange("b c f -> (b c) f")
+        x_sb = []
+        for h in range(2):
+            x_half = keep.tile([P, NODES * STEPS], BF16, name="x_half%d" % h)
+            x_sb.append(x_half)
+        w_words = []
+        w_planes = []
+        for s in range(2):
+            words = keep.tile([P, NODES], U32, name="w_words%d" % s, align_bytes=64)
+            plane = keep.tile([P, NODES], U8, name="w_plane%d" % s, align_bytes=64)
+            nc.vector.memset(plane[:].bitcast(I32), 0)
+            w_words.append(words)
+            w_planes.append(plane)
+
+        def load_x(h):
+            half = NODES * STEPS // 2
+            for part in range(2):
+                cols = slice(part * half, (part + 1) * half)
+                nc.sync.dma_start(out=x_sb[h][:, cols], in_=x_rows[h * P : (h + 1) * P, cols])
+
+        load_x(0)
+        for s in range(2):
+            nc.sync.dma_start(
+                out=w_words[s][:].bitcast(I32),
+                in_=words_in[s][0].rearrange("p n t -> p (n t)").bitcast(I32),
+            )
+        for s in range(2):
+            for quad in range(4):
+                nc.sync.dma_start(
+                    out=w_planes[s][32 * quad : 32 * quad + 4, :].bitcast(I32),
+                    in_=scales_in[s][0, 4 * quad : 4 * quad + 4, :].bitcast(I32),
+                )
+        load_x(1)
+
+        ident = keep.tile([P, P], F32, name="ident")
+        make_identity(nc, ident[:])
+        sort_channels = keep.tile([P, P], F32, name="sort_channels")
+        nc.vector.tensor_copy(
+            out=sort_channels[:].rearrange("p (b i c) -> p b i c", b=2, i=TILES, c=CQ),
+            in_=ident[:].rearrange("p (b c i) -> p b i c", b=2, c=CQ, i=TILES),
+        )
+
+        x_banks = {}
+        x_grouped = {}
+        x_codes = {}
+        x_scales = {}
+
+        def transpose_x(g, pool, tag):
+            h, l2 = divmod(g, 8)
+            x_words = x_sb[h][:].bitcast(F32)
+            bank = pool.tile([P, PACK, P], F32, name="x_bank%d" % g, tag=tag)
+            for t in range(PACK):
+                nc.tensor.transpose(
+                    bank[:, t, :], x_words[:, 8 * t + l2 : X_WORDS : 32], sort_channels[:]
+                )
+            x_banks[g] = bank
+
+        def regroup_x(g, copy):
+            quarter, q = divmod(g, 4)
+            if q == 0:
+                x_grouped[quarter] = stage.tile(
+                    [P, 2 * TILES * P * PACK], BF16, name="x_grouped%d" % quarter,
+                    tag="x_grouped", align_bytes=64,
+                )
+            copy(
+                out=x_grouped[quarter][:].rearrange(
+                    "p (j q e t) -> p j q e t", j=P, q=4, e=2, t=PACK
+                )[:, :, q, :, :],
+                in_=x_banks[g][:]
+                .rearrange("p t j -> p (t j)")
+                .bitcast(BF16)
+                .rearrange("p (t j e) -> p j e t", t=PACK, j=P, e=2),
+            )
+
+        def quantise_x(quarter):
+            codes = stage.tile(
+                [P, 2 * TILES * P], U32, name="x_codes%d" % quarter, tag="x_codes", align_bytes=64
+            )
+            scales = stage.tile(
+                [P, 2 * TILES * P], U8, name="x_scales%d" % quarter, tag="x_scales", align_bytes=64
+            )
+            nc.vector.quantize_mx(
+                out=codes[:].bitcast(FP8X4), scales=scales[:], in_=x_grouped[quarter][:]
+            )
+            x_codes[quarter] = codes
+            x_scales[quarter] = scales
+
+        hop1_bf16 = {}
+        flipped = {}
+        hop1_codes = {}
+        hop1_scales = {}
+
+        def place(u):
+            quarter, rest = divmod(u, 4)
+            b_lo, s = divmod(rest, 2)
+            return quarter, b_lo, s
+
+        def four_passes(u, codes, scales, first_col, out_view, tag):
+            quarter, b_lo, s = place(u)
+            h, lh = divmod(quarter, 2)
+            rows = rows_pool.tile([P, TILES, NODES], F32, name="%s%d" % (tag, u), tag=tag)
+            for i in range(TILES):
+                cols = slice(first_col + i * P, first_col + (i + 1) * P)
+                acc = acc_pool.tile([P, NODES], F32, name="acc_%s%d_%d" % (tag, u, i), tag="acc")
+                nc.tensor.matmul_mx(
+                    out=acc[:],
+                    lhsT=codes[:, cols].bitcast(FP8X4),
+                    lhsT_scale=scales[:, cols],
+                    rhs=w_words[s][:].bitcast(FP8X4),
+                    rhs_scale=w_planes[s][:],
+                    start=True,
+                    stop=True,
+                )
+                nc.scalar.copy(out=rows[:, i, :], in_=acc[:])
+            nc.sync.dma_start(
+                out=out_view[s][2 * h + b_lo, lh], in_=rows[:].rearrange("m i w -> m (i w)")
+            )
+            return rows
+
+        def first_hop(u):
+            quarter, b_lo, s = place(u)
+            rows = four_passes(
+                u, x_codes[quarter], x_scales[quarter], b_lo * TILES * P, hop1_out, "hop1_rows"
+            )
+            rounded = stage.tile([P, TILES, NODES], BF16, name="hop1_bf16_%d" % u, tag="hop1_bf16")
+            nc.vector.tensor_copy(out=rounded[:], in_=rows[:])
+            hop1_bf16[u] = rounded
+
+        def transpose_hop1(u):
+            flipped[u] = []
+            for pair in range(TILES // 2):
+                bank = flip_pool.tile([P, 2, 2, P], F32, name="flip%d_%d" % (u, pair), tag="flip")
+                for i in range(2):
+                    node_pairs = hop1_bf16[u][:, 2 * pair + i, :].bitcast(F32)
+                    for half in range(2):
+                        nc.tensor.transpose(
+                            bank[:, i, half, :], node_pairs[:, half : NODES // 2 : 2], ident[:]
+                        )
+                flipped[u].append(bank)
+
+        def regroup_hop1(u):
+            grouped = stage.tile(
+                [P, TILES * P * PACK], BF16, name="hop1_grouped%d" % u, tag="hop1_grouped",
+                align_bytes=64,
+            )
+            as_words = grouped[:].bitcast(F32).rearrange(
+                "p (i m half) -> p i m half", i=TILES, m=P, half=2
+            )
+            for pair in range(TILES // 2):
+                nc.vector.tensor_copy(
+                    out=as_words[:, 2 * pair : 2 * pair + 2, :, :],
+                    in_=flipped[u][pair][:].rearrange("p i half m -> p i m half"),
+                )
+            return grouped
+
+        def quantise_hop1(u, grouped):
+            codes = stage.tile(
+                [P, TILES * P], U32, name="hop1_codes%d" % u, tag="hop1_codes", align_bytes=64
+            )
+            scales = stage.tile(
+                [P, TILES * P], U8, name="hop1_scales%d" % u, tag="hop1_scales", align_bytes=64
+            )
+            nc.vector.quantize_mx(out=codes[:].bitcast(FP8X4), scales=scales[:], in_=grouped[:])
+            hop1_codes[u] = codes
+            hop1_scales[u] = scales
+
+        for g in (0, 2, 1, 3):
+            transpose_x(g, acc_pool, "acc")
+        regroup_x(0, nc.vector.tensor_copy)
+        regroup_x(2, nc.scalar.copy)
+        regroup_x(1, nc.vector.tensor_copy)
+        regroup_x(3, nc.scalar.copy)
+        quantise_x(0)
+
+        for n in range(4 - X_LEAD - 1, UNITS + HOP2_LAG):
+            u_quant = n - QUANTISE_LAG
+            g_out = n + X_LEAD
+            grouped = regroup_hop1(u_quant) if 0 <= u_quant < UNITS else None
+            if 4 <= g_out < X_BANKS:
+                regroup_x(g_out, nc.vector.tensor_copy)
+            if grouped is not None:
+                quantise_hop1(u_quant, grouped)
+            if 0 <= n < UNITS:
+                first_hop(n)
+            if 4 <= g_out < X_BANKS and g_out % 4 == 3:
+                quantise_x(g_out // 4)
+            u_hop2 = n - HOP2_LAG
+            if 0 <= u_hop2 < UNITS:
+                four_passes(u_hop2, hop1_codes[u_hop2], hop1_scales[u_hop2], 0, hop2_out, "hop2_rows")
+            if 0 <= n - TRANSPOSE_LAG < UNITS:
+                transpose_hop1(n - TRANSPOSE_LAG)
+            if 4 <= g_out + 1 < X_BANKS:
+                transpose_x(g_out + 1, flip_pool, "flip")

@@ -246,10 +246,10 @@ def tile_adaptivegcn_pb_t_kernel(
                 first_hop(n)
             if 4 <= g_out < X_BANKS and g_out % 4 == 3:
                 quantise_x(g_out // 4)
+            if 0 <= n - TRANSPOSE_LAG < UNITS:
+                transpose_hop1(n - TRANSPOSE_LAG)
             u_hop2 = n - HOP2_LAG
             if 0 <= u_hop2 < UNITS:
                 four_passes(u_hop2, hop1_codes[u_hop2], hop1_scales[u_hop2], 0, hop2_out, "hop2_rows")
-            if 0 <= n - TRANSPOSE_LAG < UNITS:
-                transpose_hop1(n - TRANSPOSE_LAG)
             if 4 <= g_out + 1 < X_BANKS:
                 transpose_x(g_out + 1, flip_pool, "flip")

@@ -185,7 +185,14 @@ def tile_adaptivegcn_pb_t_kernel(
                 u, x_codes[quarter], x_scales[quarter], b_lo * TILES * P, hop1_out, "hop1_rows"
             )
             rounded = stage.tile([P, TILES, NODES], BF16, name="hop1_bf16_%d" % u, tag="hop1_bf16")
-            nc.vector.tensor_copy(out=rounded[:], in_=rows[:])
+            nc.gpsimd.tensor_scalar(
+                out=rounded[:],
+                in0=rows[:],
+                scalar1=1.0,
+                scalar2=0.0,
+                op0=mybir.AluOpType.mult,
+                op1=mybir.AluOpType.add,
+            )
             hop1_bf16[u] = rounded
 
         def transpose_hop1(u):
@@ -246,10 +253,10 @@ def tile_adaptivegcn_pb_t_kernel(
                 first_hop(n)
             if 4 <= g_out < X_BANKS and g_out % 4 == 3:
                 quantise_x(g_out // 4)
-            if 0 <= n - TRANSPOSE_LAG < UNITS:
-                transpose_hop1(n - TRANSPOSE_LAG)
             u_hop2 = n - HOP2_LAG
             if 0 <= u_hop2 < UNITS:
                 four_passes(u_hop2, hop1_codes[u_hop2], hop1_scales[u_hop2], 0, hop2_out, "hop2_rows")
+            if 0 <= n - TRANSPOSE_LAG < UNITS:
+                transpose_hop1(n - TRANSPOSE_LAG)
             if 4 <= g_out + 1 < X_BANKS:
                 transpose_x(g_out + 1, flip_pool, "flip")

@@ -173,7 +173,10 @@ def tile_adaptivegcn_pb_t_kernel(
                     start=True,
                     stop=True,
                 )
-                nc.scalar.copy(out=rows[:, i, :], in_=acc[:])
+                if i < TILES - 1:
+                    nc.scalar.copy(out=rows[:, i, :], in_=acc[:])
+                else:
+                    nc.vector.tensor_copy(out=rows[:, i, :], in_=acc[:])
             nc.sync.dma_start(
                 out=out_view[s][2 * h + b_lo, lh], in_=rows[:].rearrange("m i w -> m (i w)")
             )

@@ -45,8 +45,8 @@ def tile_adaptivegcn_pb_t_kernel(
     scales_in = (support0_scales, support1_scales)
 
     def by_group(out):
-        return out.rearrange(
-            "(b lh ll) (cq i) w -> b lh cq ll (i w)", b=BATCH, lh=2, ll=LL, cq=CQ, i=TILES
+        return out.rearrange("n c w -> (n c) w").rearrange(
+            "(g m i) w -> g m (i w)", g=2 * BATCH, m=P, i=TILES
         )
 
     hop1_out = (by_group(out_0), by_group(out_2))
@@ -124,15 +124,17 @@ def tile_adaptivegcn_pb_t_kernel(
                     [P, 2 * TILES * P * PACK], BF16, name="x_grouped%d" % quarter,
                     tag="x_grouped", align_bytes=64,
                 )
-            copy(
-                out=x_grouped[quarter][:].rearrange(
-                    "p (j q e t) -> p j q e t", j=P, q=4, e=2, t=PACK
-                )[:, :, q, :, :],
-                in_=x_banks[g][:]
+            by_step = x_grouped[quarter][:].rearrange(
+                "p (r q e c t) -> p q e r c t", r=2 * TILES, q=4, e=2, c=CQ, t=PACK
+            )
+            bank_by_step = (
+                x_banks[g][:]
                 .rearrange("p t j -> p (t j)")
                 .bitcast(BF16)
-                .rearrange("p (t j e) -> p j e t", t=PACK, j=P, e=2),
+                .rearrange("p (t r c e) -> p e r c t", t=PACK, r=2 * TILES, c=CQ, e=2)
             )
+            for e in range(2):
+                copy(out=by_step[:, q, e], in_=bank_by_step[:, e])
 
         def quantise_x(quarter):
             codes = stage.tile(
@@ -178,7 +180,7 @@ def tile_adaptivegcn_pb_t_kernel(
                 else:
                     nc.vector.tensor_copy(out=rows[:, i, :], in_=acc[:])
             nc.sync.dma_start(
-                out=out_view[s][2 * h + b_lo, lh], in_=rows[:].rearrange("m i w -> m (i w)")
+                out=out_view[s][2 * (2 * h + b_lo) + lh], in_=rows[:].rearrange("m i w -> m (i w)")
             )
             return rows
 

@@ -23,39 +23,33 @@ X_WORDS = NODES * STEPS // 2
 TRANSPOSE_LAG = 1
 QUANTISE_LAG = 2
 HOP2_LAG = 3
-X_LEAD = 5
+X_LEAD = 4
+BURST = 5
 
 FLOPS = 4 * 2 * BATCH * STEPS * CHANNELS * NODES * NODES
 
 
+ROW_BUFS = 14
+SPLIT_ROUND = True
+
+
 def tile_adaptivegcn_pb_t_kernel(
-    tc,
-    x,
-    support0_words,
-    support0_scales,
-    support1_words,
-    support1_scales,
-    out_0,
-    out_1,
-    out_2,
-    out_3,
+    tc, x, support0_words, support0_scales, support1_words, support1_scales, out_0, out_1, out_2, out_3
 ):
     nc = tc.nc
     words_in = (support0_words, support1_words)
     scales_in = (support0_scales, support1_scales)
 
     def by_group(out):
-        return out.rearrange("n c w -> (n c) w").rearrange(
-            "(g m i) w -> g m (i w)", g=2 * BATCH, m=P, i=TILES
-        )
+        return out.rearrange("n c w -> (n c) w").rearrange("(g m i) w -> g m (i w)", g=2 * BATCH, m=P, i=TILES)
 
     hop1_out = (by_group(out_0), by_group(out_2))
     hop2_out = (by_group(out_1), by_group(out_3))
 
     with ExitStack() as stack:
         keep = stack.enter_context(tc.tile_pool(name="keep", bufs=1))
-        stage = stack.enter_context(tc.tile_pool(name="stage", bufs=2))
-        rows_pool = stack.enter_context(tc.tile_pool(name="rows", bufs=4))
+        stage = stack.enter_context(tc.tile_pool(name="stage", bufs=3))
+        rows_pool = stack.enter_context(tc.tile_pool(name="rows", bufs=ROW_BUFS))
         acc_pool = stack.enter_context(tc.psum_pool(name="acc", bufs=5))
         flip_pool = stack.enter_context(tc.psum_pool(name="flip", bufs=3))
         stack.enter_context(tc.manual_schedule())
@@ -83,8 +77,7 @@ def tile_adaptivegcn_pb_t_kernel(
         load_x(0)
         for s in range(2):
             nc.sync.dma_start(
-                out=w_words[s][:].bitcast(I32),
-                in_=words_in[s][0].rearrange("p n t -> p (n t)").bitcast(I32),
+                out=w_words[s][:].bitcast(I32), in_=words_in[s][0].rearrange("p n t -> p (n t)").bitcast(I32)
             )
         for s in range(2):
             for quad in range(4):
@@ -102,6 +95,12 @@ def tile_adaptivegcn_pb_t_kernel(
             in_=ident[:].rearrange("p (b c i) -> p b i c", b=2, c=CQ, i=TILES),
         )
 
+        def evac(engine, out, in_):
+            if engine == "V":
+                nc.vector.tensor_copy(out=out, in_=in_)
+            else:
+                nc.scalar.copy(out=out, in_=in_)
+
         x_banks = {}
         x_grouped = {}
         x_codes = {}
@@ -112,93 +111,68 @@ def tile_adaptivegcn_pb_t_kernel(
             x_words = x_sb[h][:].bitcast(F32)
             bank = pool.tile([P, PACK, P], F32, name="x_bank%d" % g, tag=tag)
             for t in range(PACK):
-                nc.tensor.transpose(
-                    bank[:, t, :], x_words[:, 8 * t + l2 : X_WORDS : 32], sort_channels[:]
-                )
+                nc.tensor.transpose(bank[:, t, :], x_words[:, 8 * t + l2 : X_WORDS : 32], sort_channels[:])
             x_banks[g] = bank
 
-        def regroup_x(g, copy):
+        def regroup_x(g, b_lo, engine):
             quarter, q = divmod(g, 4)
+            j = 2 * quarter + b_lo
             if q == 0:
-                x_grouped[quarter] = stage.tile(
-                    [P, 2 * TILES * P * PACK], BF16, name="x_grouped%d" % quarter,
-                    tag="x_grouped", align_bytes=64,
+                x_grouped[j] = stage.tile(
+                    [P, TILES * P * PACK], BF16, name="x_grouped%d" % j, tag="x_grouped", align_bytes=64
                 )
-            by_step = x_grouped[quarter][:].rearrange(
-                "p (r q e c t) -> p q e r c t", r=2 * TILES, q=4, e=2, c=CQ, t=PACK
-            )
-            bank_by_step = (
+            dst = x_grouped[j][:].rearrange("p (i q e c t) -> p q i e c t", i=TILES, q=4, e=2, c=CQ, t=PACK)
+            src = (
                 x_banks[g][:]
                 .rearrange("p t j -> p (t j)")
                 .bitcast(BF16)
-                .rearrange("p (t r c e) -> p e r c t", t=PACK, r=2 * TILES, c=CQ, e=2)
+                .rearrange("p (t b i c e) -> p b i e c t", t=PACK, b=2, i=TILES, c=CQ, e=2)
             )
-            for e in range(2):
-                copy(out=by_step[:, q, e], in_=bank_by_step[:, e])
+            evac(engine, dst[:, q], src[:, b_lo])
 
-        def quantise_x(quarter):
-            codes = stage.tile(
-                [P, 2 * TILES * P], U32, name="x_codes%d" % quarter, tag="x_codes", align_bytes=64
-            )
-            scales = stage.tile(
-                [P, 2 * TILES * P], U8, name="x_scales%d" % quarter, tag="x_scales", align_bytes=64
-            )
-            nc.vector.quantize_mx(
-                out=codes[:].bitcast(FP8X4), scales=scales[:], in_=x_grouped[quarter][:]
-            )
-            x_codes[quarter] = codes
-            x_scales[quarter] = scales
+        def quantise_x(j):
+            codes = stage.tile([P, TILES * P], U32, name="x_codes%d" % j, tag="x_codes", align_bytes=64)
+            scales = stage.tile([P, TILES * P], U8, name="x_scales%d" % j, tag="x_scales", align_bytes=64)
+            nc.vector.quantize_mx(out=codes[:].bitcast(FP8X4), scales=scales[:], in_=x_grouped[j][:])
+            x_codes[j] = codes
+            x_scales[j] = scales
 
+        hop1_rows = {}
         hop1_bf16 = {}
         flipped = {}
+        hop1_grouped = {}
         hop1_codes = {}
         hop1_scales = {}
 
-        def place(u):
-            quarter, rest = divmod(u, 4)
-            b_lo, s = divmod(rest, 2)
-            return quarter, b_lo, s
-
-        def four_passes(u, codes, scales, first_col, out_view, tag):
-            quarter, b_lo, s = place(u)
+        def four_passes(u, codes, scales, out_view, tag, engines, after_bank=None):
+            j, s = divmod(u, 2)
+            quarter, b_lo = divmod(j, 2)
             h, lh = divmod(quarter, 2)
-            rows = rows_pool.tile([P, TILES, NODES], F32, name="%s%d" % (tag, u), tag=tag)
+            rows = rows_pool.tile([P, TILES, NODES], F32, name="%s%d" % (tag, u), tag="rows")
             for i in range(TILES):
-                cols = slice(first_col + i * P, first_col + (i + 1) * P)
+                cols = slice(i * P, (i + 1) * P)
                 acc = acc_pool.tile([P, NODES], F32, name="acc_%s%d_%d" % (tag, u, i), tag="acc")
                 nc.tensor.matmul_mx(
-                    out=acc[:],
-                    lhsT=codes[:, cols].bitcast(FP8X4),
-                    lhsT_scale=scales[:, cols],
-                    rhs=w_words[s][:].bitcast(FP8X4),
-                    rhs_scale=w_planes[s][:],
-                    start=True,
-                    stop=True,
+                    out=acc[:], lhsT=codes[:, cols].bitcast(FP8X4), lhsT_scale=scales[:, cols],
+                    rhs=w_words[s][:].bitcast(FP8X4), rhs_scale=w_planes[s][:], start=True, stop=True,
                 )
-                if i < TILES - 1:
-                    nc.scalar.copy(out=rows[:, i, :], in_=acc[:])
-                else:
-                    nc.vector.tensor_copy(out=rows[:, i, :], in_=acc[:])
-            nc.sync.dma_start(
-                out=out_view[s][2 * (2 * h + b_lo) + lh], in_=rows[:].rearrange("m i w -> m (i w)")
-            )
+                evac(engines[i], rows[:, i, :], acc[:])
+                if after_bank is not None:
+                    after_bank(rows, i)
+            nc.sync.dma_start(out=out_view[s][2 * (2 * h + b_lo) + lh], in_=rows[:].rearrange("m i w -> m (i w)"))
             return rows
 
-        def first_hop(u):
-            quarter, b_lo, s = place(u)
-            rows = four_passes(
-                u, x_codes[quarter], x_scales[quarter], b_lo * TILES * P, hop1_out, "hop1_rows"
-            )
+        def first_hop(u, engines):
             rounded = stage.tile([P, TILES, NODES], BF16, name="hop1_bf16_%d" % u, tag="hop1_bf16")
-            nc.gpsimd.tensor_scalar(
-                out=rounded[:],
-                in0=rows[:],
-                scalar1=1.0,
-                scalar2=0.0,
-                op0=mybir.AluOpType.mult,
-                op1=mybir.AluOpType.add,
-            )
             hop1_bf16[u] = rounded
+
+            def round_tile(rows, i):
+                nc.gpsimd.tensor_scalar(
+                    out=rounded[:, i, :], in0=rows[:, i, :], scalar1=1.0, scalar2=0.0,
+                    op0=mybir.AluOpType.mult, op1=mybir.AluOpType.add,
+                )
+
+            four_passes(u, x_codes[u // 2], x_scales[u // 2], hop1_out, "hop1_rows", engines, round_tile)
 
         def transpose_hop1(u):
             flipped[u] = []
@@ -207,60 +181,96 @@ def tile_adaptivegcn_pb_t_kernel(
                 for i in range(2):
                     node_pairs = hop1_bf16[u][:, 2 * pair + i, :].bitcast(F32)
                     for half in range(2):
-                        nc.tensor.transpose(
-                            bank[:, i, half, :], node_pairs[:, half : NODES // 2 : 2], ident[:]
-                        )
+                        nc.tensor.transpose(bank[:, i, half, :], node_pairs[:, half : NODES // 2 : 2], ident[:])
                 flipped[u].append(bank)
 
-        def regroup_hop1(u):
+        def regroup_hop1(u, engines):
             grouped = stage.tile(
-                [P, TILES * P * PACK], BF16, name="hop1_grouped%d" % u, tag="hop1_grouped",
-                align_bytes=64,
+                [P, TILES * P * PACK], BF16, name="hop1_grouped%d" % u, tag="hop1_grouped", align_bytes=64
             )
-            as_words = grouped[:].bitcast(F32).rearrange(
-                "p (i m half) -> p i m half", i=TILES, m=P, half=2
-            )
+            as_words = grouped[:].bitcast(F32).rearrange("p (i m half) -> p i m half", i=TILES, m=P, half=2)
             for pair in range(TILES // 2):
-                nc.vector.tensor_copy(
-                    out=as_words[:, 2 * pair : 2 * pair + 2, :, :],
-                    in_=flipped[u][pair][:].rearrange("p i half m -> p i m half"),
+                evac(
+                    engines[pair], as_words[:, 2 * pair : 2 * pair + 2, :, :],
+                    flipped[u][pair][:].rearrange("p i half m -> p i m half"),
                 )
-            return grouped
+            hop1_grouped[u] = grouped
 
-        def quantise_hop1(u, grouped):
-            codes = stage.tile(
-                [P, TILES * P], U32, name="hop1_codes%d" % u, tag="hop1_codes", align_bytes=64
-            )
-            scales = stage.tile(
-                [P, TILES * P], U8, name="hop1_scales%d" % u, tag="hop1_scales", align_bytes=64
-            )
-            nc.vector.quantize_mx(out=codes[:].bitcast(FP8X4), scales=scales[:], in_=grouped[:])
+        def quantise_hop1(u):
+            codes = stage.tile([P, TILES * P], U32, name="hop1_codes%d" % u, tag="hop1_codes", align_bytes=64)
+            scales = stage.tile([P, TILES * P], U8, name="hop1_scales%d" % u, tag="hop1_scales", align_bytes=64)
+            nc.vector.quantize_mx(out=codes[:].bitcast(FP8X4), scales=scales[:], in_=hop1_grouped[u][:])
             hop1_codes[u] = codes
             hop1_scales[u] = scales
 
-        for g in (0, 2, 1, 3):
-            transpose_x(g, acc_pool, "acc")
-        regroup_x(0, nc.vector.tensor_copy)
-        regroup_x(2, nc.scalar.copy)
-        regroup_x(1, nc.vector.tensor_copy)
-        regroup_x(3, nc.scalar.copy)
-        quantise_x(0)
+        def second_hop(u, engines):
+            four_passes(u, hop1_codes[u], hop1_scales[u], hop2_out, "hop2_rows", engines)
 
-        for n in range(4 - X_LEAD - 1, UNITS + HOP2_LAG):
+        def regroup_x_bank(g, engine):
+            regroup_x(g, 0, engine)
+            regroup_x(g, 1, engine)
+
+        for g in (0, 1, 2):
+            transpose_x(g, flip_pool, "flip")
+        transpose_x(3, acc_pool, "acc")
+        for g in range(4):
+            regroup_x_bank(g, "VS"[g % 2])
+            if g % 2 == 1:
+                transpose_x(4 + g // 2, flip_pool, "flip")
+        quantise_x(0)
+        quantise_x(1)
+        regroup_x(4, 0, "S")
+        first_hop(0, "VSVS")
+        regroup_x(4, 1, "S")
+        first_hop(1, "VSVS")
+        transpose_x(6, flip_pool, "flip")
+        regroup_x_bank(5, "V")
+        first_hop(2, "SVSS")
+        transpose_hop1(0)
+        regroup_x_bank(6, "S")
+        first_hop(3, "VVSV")
+        transpose_x(7, flip_pool, "flip")
+        regroup_hop1(0, "VS")
+        transpose_hop1(1)
+        regroup_x_bank(7, "S")
+        quantise_hop1(0)
+        regroup_hop1(1, "VS")
+        quantise_x(2)
+        second_hop(0, "SVSV")
+        first_hop(4, "SVSV")
+        transpose_x(8, flip_pool, "flip")
+        transpose_hop1(2)
+        quantise_hop1(1)
+        for n in range(4, UNITS + HOP2_LAG):
             u_quant = n - QUANTISE_LAG
-            g_out = n + X_LEAD
-            grouped = regroup_hop1(u_quant) if 0 <= u_quant < UNITS else None
-            if 4 <= g_out < X_BANKS:
-                regroup_x(g_out, nc.vector.tensor_copy)
-            if grouped is not None:
-                quantise_hop1(u_quant, grouped)
-            if 0 <= n < UNITS:
-                first_hop(n)
-            if 4 <= g_out < X_BANKS and g_out % 4 == 3:
-                quantise_x(g_out // 4)
             u_hop2 = n - HOP2_LAG
+            g_out = n + X_LEAD
+            has_q = 0 <= u_quant < UNITS
+            has_x = 4 <= g_out < X_BANKS
+            has_h1 = BURST <= n < UNITS
+            quants = [j for j in range(3, 8) if (2 * j - 1 if j % 2 == 0 else 2 * j - 2) * (j > 1) == n]
+            products = (TILES if has_h1 else 0) + (TILES if 0 <= u_hop2 < UNITS else 0)
+            copies = 2 * has_q + 2 * has_x + products
+            v_copies = max(0, (copies - has_q - len(quants)) // 2)
+            small = 2 * has_q + 2 * has_x
+            small_engines = "V" * min(small, v_copies) + "S" * max(0, small - v_copies)
+            n_v = max(0, v_copies - small)
+            engines = ["S"] * (products - n_v) + ["V"] * n_v
+            if has_q:
+                regroup_hop1(u_quant, small_engines[:2])
+                small_engines = small_engines[2:]
+            if has_x:
+                regroup_x(g_out, 0, small_engines[0])
+                regroup_x(g_out, 1, small_engines[1])
+            if has_q:
+                quantise_hop1(u_quant)
+            for j in quants:
+                quantise_x(j)
+            if has_h1:
+                first_hop(n, engines[:TILES])
+                engines = engines[TILES:]
             if 0 <= u_hop2 < UNITS:
-                four_passes(u_hop2, hop1_codes[u_hop2], hop1_scales[u_hop2], 0, hop2_out, "hop2_rows")
+                four_passes(u_hop2, hop1_codes[u_hop2], hop1_scales[u_hop2], hop2_out, "hop2_rows", engines)
             if 0 <= n - TRANSPOSE_LAG < UNITS:
                 transpose_hop1(n - TRANSPOSE_LAG)
             if 4 <= g_out + 1 < X_BANKS:

@@ -166,13 +166,10 @@ def tile_adaptivegcn_pb_t_kernel(
             rounded = stage.tile([P, TILES, NODES], BF16, name="hop1_bf16_%d" % u, tag="hop1_bf16")
             hop1_bf16[u] = rounded
 
-            def round_tile(rows, i):
-                nc.gpsimd.tensor_scalar(
-                    out=rounded[:, i, :], in0=rows[:, i, :], scalar1=1.0, scalar2=0.0,
-                    op0=mybir.AluOpType.mult, op1=mybir.AluOpType.add,
-                )
+            hop1_rows[u] = four_passes(u, x_codes[u // 2], x_scales[u // 2], hop1_out, "hop1_rows", engines)
 
-            four_passes(u, x_codes[u // 2], x_scales[u // 2], hop1_out, "hop1_rows", engines, round_tile)
+        def round_hop1(u):
+            nc.vector.tensor_copy(out=hop1_bf16[u][:], in_=hop1_rows[u][:])
 
         def transpose_hop1(u):
             flipped[u] = []
@@ -223,18 +220,21 @@ def tile_adaptivegcn_pb_t_kernel(
         first_hop(0, "VSVS")
         regroup_x(4, 1, "S")
         first_hop(1, "VSVS")
+        round_hop1(0)
         transpose_x(6, flip_pool, "flip")
-        regroup_x_bank(5, "V")
-        first_hop(2, "SVSS")
+        regroup_x_bank(5, "S")
+        first_hop(2, "VSVS")
         transpose_hop1(0)
+        round_hop1(1)
         regroup_x_bank(6, "S")
-        first_hop(3, "VVSV")
+        first_hop(3, "VSVS")
         transpose_x(7, flip_pool, "flip")
         regroup_hop1(0, "VS")
         transpose_hop1(1)
         regroup_x_bank(7, "S")
         quantise_hop1(0)
-        regroup_hop1(1, "VS")
+        round_hop1(2)
+        regroup_hop1(1, "SS")
         quantise_x(2)
         second_hop(0, "SVSV")
         first_hop(4, "SVSV")
@@ -251,11 +251,14 @@ def tile_adaptivegcn_pb_t_kernel(
             quants = [j for j in range(3, 8) if (2 * j - 1 if j % 2 == 0 else 2 * j - 2) * (j > 1) == n]
             products = (TILES if has_h1 else 0) + (TILES if 0 <= u_hop2 < UNITS else 0)
             copies = 2 * has_q + 2 * has_x + products
-            v_copies = max(0, (copies - has_q - len(quants)) // 2)
+            has_r = 0 <= n - 1 < UNITS
+            v_copies = max(0, (copies - has_q - len(quants) - 2 * has_r) // 2)
             small = 2 * has_q + 2 * has_x
             small_engines = "V" * min(small, v_copies) + "S" * max(0, small - v_copies)
             n_v = max(0, v_copies - small)
             engines = ["S"] * (products - n_v) + ["V"] * n_v
+            if has_r:
+                round_hop1(n - 1)
             if has_q:
                 regroup_hop1(u_quant, small_engines[:2])
                 small_engines = small_engines[2:]

@@ -169,7 +169,10 @@ def tile_adaptivegcn_pb_t_kernel(
             hop1_rows[u] = four_passes(u, x_codes[u // 2], x_scales[u // 2], hop1_out, "hop1_rows", engines)
 
         def round_hop1(u):
-            nc.vector.tensor_copy(out=hop1_bf16[u][:], in_=hop1_rows[u][:])
+            nc.vector.tensor_copy(
+                out=hop1_bf16[u][:].rearrange("p i (half j e) -> p i half j e", half=2, j=P, e=2),
+                in_=hop1_rows[u][:].rearrange("p i (j half e) -> p i half j e", j=P, half=2, e=2),
+            )
 
         def transpose_hop1(u):
             flipped[u] = []
@@ -178,7 +181,7 @@ def tile_adaptivegcn_pb_t_kernel(
                 for i in range(2):
                     node_pairs = hop1_bf16[u][:, 2 * pair + i, :].bitcast(F32)
                     for half in range(2):
-                        nc.tensor.transpose(bank[:, i, half, :], node_pairs[:, half : NODES // 2 : 2], ident[:])
+                        nc.tensor.transpose(bank[:, i, half, :], node_pairs[:, half * P : (half + 1) * P], ident[:])
                 flipped[u].append(bank)
 
         def regroup_hop1(u, engines):

@@ -30,6 +30,7 @@ FLOPS = 4 * 2 * BATCH * STEPS * CHANNELS * NODES * NODES
 
 
 ROW_BUFS = 14
+WARM_UP = 16
 SPLIT_ROUND = True
 
 
@@ -86,6 +87,12 @@ def tile_adaptivegcn_pb_t_kernel(
                     in_=scales_in[s][0, 4 * quad : 4 * quad + 4, :].bitcast(I32),
                 )
         load_x(1)
+
+        warm = keep.tile([P, NODES], BF16, name="warm")
+        nc.vector.memset(warm[:], 0.0)
+        warm_out = acc_pool.tile([P, NODES], F32, name="warm_out", tag="acc")
+        for k in range(WARM_UP):
+            nc.tensor.matmul(out=warm_out[:], lhsT=warm[:, :P], rhs=warm[:], start=True, stop=True)
 
         ident = keep.tile([P, P], F32, name="ident")
         make_identity(nc, ident[:])

@@ -9,6 +9,8 @@ I32 = mybir.dt.int32
 U32 = mybir.dt.uint32
 U8 = mybir.dt.uint8
 FP8X4 = mybir.dt.float8_e4m3fn_x4
+MULT = mybir.AluOpType.mult
+ADD = mybir.AluOpType.add
 
 P = 128
 PACK = 4
@@ -91,8 +93,11 @@ def tile_adaptivegcn_pb_t_kernel(
         warm = keep.tile([P, NODES], BF16, name="warm")
         nc.vector.memset(warm[:], 0.0)
         warm_out = acc_pool.tile([P, NODES], F32, name="warm_out", tag="acc")
-        for k in range(WARM_UP):
-            nc.tensor.matmul(out=warm_out[:], lhsT=warm[:, :P], rhs=warm[:], start=True, stop=True)
+        def keep_warm(count):
+            for k in range(count):
+                nc.tensor.matmul(out=warm_out[:], lhsT=warm[:, :P], rhs=warm[:], start=True, stop=True)
+
+        keep_warm(WARM_UP)
 
         ident = keep.tile([P, P], F32, name="ident")
         make_identity(nc, ident[:])
@@ -175,6 +180,15 @@ def tile_adaptivegcn_pb_t_kernel(
 
             hop1_rows[u] = four_passes(u, x_codes[u // 2], x_scales[u // 2], hop1_out, "hop1_rows", engines)
 
+        in_order = set()
+
+        def round_on_gpsimd(u):
+            nc.gpsimd.tensor_scalar(
+                out=hop1_bf16[u][:].rearrange("p i w -> p (i w)"), in0=hop1_rows[u][:].rearrange("p i w -> p (i w)"),
+                scalar1=1.0, scalar2=0.0, op0=MULT, op1=ADD,
+            )
+            in_order.add(u)
+
         def round_hop1(u):
             nc.vector.tensor_copy(
                 out=hop1_bf16[u][:].rearrange("p i (half j e) -> p i half j e", half=2, j=P, e=2),
@@ -188,7 +202,8 @@ def tile_adaptivegcn_pb_t_kernel(
                 for i in range(2):
                     node_pairs = hop1_bf16[u][:, 2 * pair + i, :].bitcast(F32)
                     for half in range(2):
-                        nc.tensor.transpose(bank[:, i, half, :], node_pairs[:, half * P : (half + 1) * P], ident[:])
+                        words = slice(half, 2 * P, 2) if u in in_order else slice(half * P, (half + 1) * P)
+                        nc.tensor.transpose(bank[:, i, half, :], node_pairs[:, words], ident[:])
                 flipped[u].append(bank)
 
         def regroup_hop1(u, engines):
@@ -220,6 +235,11 @@ def tile_adaptivegcn_pb_t_kernel(
         for g in (0, 1, 2):
             transpose_x(g, flip_pool, "flip")
         transpose_x(3, acc_pool, "acc")
+        for k in range(2):
+            nc.tensor.matmul_mx(
+                out=warm_out[:], lhsT=w_words[0][:, :P].bitcast(FP8X4), lhsT_scale=w_planes[0][:, :P],
+                rhs=w_words[0][:].bitcast(FP8X4), rhs_scale=w_planes[0][:], start=True, stop=True,
+            )
         for g in range(4):
             regroup_x_bank(g, "VS"[g % 2])
             if g % 2 == 1:
@@ -230,13 +250,13 @@ def tile_adaptivegcn_pb_t_kernel(
         first_hop(0, "VSVS")
         regroup_x(4, 1, "S")
         first_hop(1, "VSVS")
-        round_hop1(0)
+        round_on_gpsimd(0)
         transpose_x(6, flip_pool, "flip")
         regroup_x_bank(5, "S")
         first_hop(2, "VSVS")
         transpose_hop1(0)
-        round_hop1(1)
-        regroup_x_bank(6, "S")
+        round_on_gpsimd(1)
+        regroup_x_bank(6, "V")
         first_hop(3, "VSVS")
         transpose_x(7, flip_pool, "flip")
         regroup_hop1(0, "VS")
@@ -286,5 +306,9 @@ def tile_adaptivegcn_pb_t_kernel(
                 four_passes(u_hop2, hop1_codes[u_hop2], hop1_scales[u_hop2], hop2_out, "hop2_rows", engines)
             if 0 <= n - TRANSPOSE_LAG < UNITS:
                 transpose_hop1(n - TRANSPOSE_LAG)
+            if n == 4:
+                held = acc_pool.tile([P, NODES], F32, name="held_clock", tag="acc")
+                for k in range(2):
+                    nc.tensor.matmul(out=held[:], lhsT=warm[:, :P], rhs=warm[:], start=k == 0, stop=k == 1)
             if 4 <= g_out + 1 < X_BANKS:
                 transpose_x(g_out + 1, flip_pool, "flip")

from contextlib import ExitStack

import concourse.mybir as mybir
from concourse.masks import make_identity

F32 = mybir.dt.float32
BF16 = mybir.dt.bfloat16
I32 = mybir.dt.int32
U32 = mybir.dt.uint32
U8 = mybir.dt.uint8
FP8X4 = mybir.dt.float8_e4m3fn_x4
MULT = mybir.AluOpType.mult
ADD = mybir.AluOpType.add

P = 128
PACK = 4
BATCH, CHANNELS, NODES, STEPS = 4, 64, 512, 16
TILES = 4
CQ = CHANNELS // TILES
LL = P // CQ
UNITS = 16
X_BANKS = 16
X_WORDS = NODES * STEPS // 2

TRANSPOSE_LAG = 1
QUANTISE_LAG = 2
HOP2_LAG = 3
X_LEAD = 4
BURST = 5

FLOPS = 4 * 2 * BATCH * STEPS * CHANNELS * NODES * NODES


ROW_BUFS = 14
WARM_UP = 16
SPLIT_ROUND = True


def tile_adaptivegcn_pb_t_kernel(
    tc, x, support0_words, support0_scales, support1_words, support1_scales, out_0, out_1, out_2, out_3
):
    nc = tc.nc
    words_in = (support0_words, support1_words)
    scales_in = (support0_scales, support1_scales)

    def by_group(out):
        return out.rearrange("n c w -> (n c) w").rearrange("(g m i) w -> g m (i w)", g=2 * BATCH, m=P, i=TILES)

    hop1_out = (by_group(out_0), by_group(out_2))
    hop2_out = (by_group(out_1), by_group(out_3))

    with ExitStack() as stack:
        keep = stack.enter_context(tc.tile_pool(name="keep", bufs=1))
        stage = stack.enter_context(tc.tile_pool(name="stage", bufs=3))
        rows_pool = stack.enter_context(tc.tile_pool(name="rows", bufs=ROW_BUFS))
        acc_pool = stack.enter_context(tc.psum_pool(name="acc", bufs=5))
        flip_pool = stack.enter_context(tc.psum_pool(name="flip", bufs=3))
        stack.enter_context(tc.manual_schedule())

        x_rows = x.rearrange("b c f -> (b c) f")
        x_sb = []
        for h in range(2):
            x_half = keep.tile([P, NODES * STEPS], BF16, name="x_half%d" % h)
            x_sb.append(x_half)
        w_words = []
        w_planes = []
        for s in range(2):
            words = keep.tile([P, NODES], U32, name="w_words%d" % s, align_bytes=64)
            plane = keep.tile([P, NODES], U8, name="w_plane%d" % s, align_bytes=64)
            nc.vector.memset(plane[:].bitcast(I32), 0)
            w_words.append(words)
            w_planes.append(plane)

        def load_x(h):
            half = NODES * STEPS // 2
            for part in range(2):
                cols = slice(part * half, (part + 1) * half)
                nc.sync.dma_start(out=x_sb[h][:, cols], in_=x_rows[h * P : (h + 1) * P, cols])

        load_x(0)
        for s in range(2):
            nc.sync.dma_start(
                out=w_words[s][:].bitcast(I32), in_=words_in[s][0].rearrange("p n t -> p (n t)").bitcast(I32)
            )
        for s in range(2):
            for quad in range(4):
                nc.sync.dma_start(
                    out=w_planes[s][32 * quad : 32 * quad + 4, :].bitcast(I32),
                    in_=scales_in[s][0, 4 * quad : 4 * quad + 4, :].bitcast(I32),
                )
        load_x(1)

        warm = keep.tile([P, NODES], BF16, name="warm")
        nc.vector.memset(warm[:], 0.0)
        warm_out = acc_pool.tile([P, NODES], F32, name="warm_out", tag="acc")
        def keep_warm(count):
            for k in range(count):
                nc.tensor.matmul(out=warm_out[:], lhsT=warm[:, :P], rhs=warm[:], start=True, stop=True)

        keep_warm(WARM_UP)

        ident = keep.tile([P, P], F32, name="ident")
        make_identity(nc, ident[:])
        sort_channels = keep.tile([P, P], F32, name="sort_channels")
        nc.vector.tensor_copy(
            out=sort_channels[:].rearrange("p (b i c) -> p b i c", b=2, i=TILES, c=CQ),
            in_=ident[:].rearrange("p (b c i) -> p b i c", b=2, c=CQ, i=TILES),
        )

        def evac(engine, out, in_):
            if engine == "V":
                nc.vector.tensor_copy(out=out, in_=in_)
            else:
                nc.scalar.copy(out=out, in_=in_)

        x_banks = {}
        x_grouped = {}
        x_codes = {}
        x_scales = {}

        def transpose_x(g, pool, tag):
            h, l2 = divmod(g, 8)
            x_words = x_sb[h][:].bitcast(F32)
            bank = pool.tile([P, PACK, P], F32, name="x_bank%d" % g, tag=tag)
            for t in range(PACK):
                nc.tensor.transpose(bank[:, t, :], x_words[:, 8 * t + l2 : X_WORDS : 32], sort_channels[:])
            x_banks[g] = bank

        def regroup_x(g, b_lo, engine):
            quarter, q = divmod(g, 4)
            j = 2 * quarter + b_lo
            if q == 0:
                x_grouped[j] = stage.tile(
                    [P, TILES * P * PACK], BF16, name="x_grouped%d" % j, tag="x_grouped", align_bytes=64
                )
            dst = x_grouped[j][:].rearrange("p (i q e c t) -> p q i e c t", i=TILES, q=4, e=2, c=CQ, t=PACK)
            src = (
                x_banks[g][:]
                .rearrange("p t j -> p (t j)")
                .bitcast(BF16)
                .rearrange("p (t b i c e) -> p b i e c t", t=PACK, b=2, i=TILES, c=CQ, e=2)
            )
            evac(engine, dst[:, q], src[:, b_lo])

        def quantise_x(j):
            codes = stage.tile([P, TILES * P], U32, name="x_codes%d" % j, tag="x_codes", align_bytes=64)
            scales = stage.tile([P, TILES * P], U8, name="x_scales%d" % j, tag="x_scales", align_bytes=64)
            nc.vector.quantize_mx(out=codes[:].bitcast(FP8X4), scales=scales[:], in_=x_grouped[j][:])
            x_codes[j] = codes
            x_scales[j] = scales

        hop1_rows = {}
        hop1_bf16 = {}
        flipped = {}
        hop1_grouped = {}
        hop1_codes = {}
        hop1_scales = {}

        def four_passes(u, codes, scales, out_view, tag, engines, after_bank=None):
            j, s = divmod(u, 2)
            quarter, b_lo = divmod(j, 2)
            h, lh = divmod(quarter, 2)
            rows = rows_pool.tile([P, TILES, NODES], F32, name="%s%d" % (tag, u), tag="rows")
            for i in range(TILES):
                cols = slice(i * P, (i + 1) * P)
                acc = acc_pool.tile([P, NODES], F32, name="acc_%s%d_%d" % (tag, u, i), tag="acc")
                nc.tensor.matmul_mx(
                    out=acc[:], lhsT=codes[:, cols].bitcast(FP8X4), lhsT_scale=scales[:, cols],
                    rhs=w_words[s][:].bitcast(FP8X4), rhs_scale=w_planes[s][:], start=True, stop=True,
                )
                evac(engines[i], rows[:, i, :], acc[:])
                if after_bank is not None:
                    after_bank(rows, i)
            nc.sync.dma_start(out=out_view[s][2 * (2 * h + b_lo) + lh], in_=rows[:].rearrange("m i w -> m (i w)"))
            return rows

        def first_hop(u, engines):
            rounded = stage.tile([P, TILES, NODES], BF16, name="hop1_bf16_%d" % u, tag="hop1_bf16")
            hop1_bf16[u] = rounded

            hop1_rows[u] = four_passes(u, x_codes[u // 2], x_scales[u // 2], hop1_out, "hop1_rows", engines)

        in_order = set()

        def round_on_gpsimd(u):
            nc.gpsimd.tensor_scalar(
                out=hop1_bf16[u][:].rearrange("p i w -> p (i w)"), in0=hop1_rows[u][:].rearrange("p i w -> p (i w)"),
                scalar1=1.0, scalar2=0.0, op0=MULT, op1=ADD,
            )
            in_order.add(u)

        def round_hop1(u):
            nc.vector.tensor_copy(
                out=hop1_bf16[u][:].rearrange("p i (half j e) -> p i half j e", half=2, j=P, e=2),
                in_=hop1_rows[u][:].rearrange("p i (j half e) -> p i half j e", j=P, half=2, e=2),
            )

        def transpose_hop1(u):
            flipped[u] = []
            for pair in range(TILES // 2):
                bank = flip_pool.tile([P, 2, 2, P], F32, name="flip%d_%d" % (u, pair), tag="flip")
                for i in range(2):
                    node_pairs = hop1_bf16[u][:, 2 * pair + i, :].bitcast(F32)
                    for half in range(2):
                        words = slice(half, 2 * P, 2) if u in in_order else slice(half * P, (half + 1) * P)
                        nc.tensor.transpose(bank[:, i, half, :], node_pairs[:, words], ident[:])
                flipped[u].append(bank)

        def regroup_hop1(u, engines):
            grouped = stage.tile(
                [P, TILES * P * PACK], BF16, name="hop1_grouped%d" % u, tag="hop1_grouped", align_bytes=64
            )
            as_words = grouped[:].bitcast(F32).rearrange("p (i m half) -> p i m half", i=TILES, m=P, half=2)
            for pair in range(TILES // 2):
                evac(
                    engines[pair], as_words[:, 2 * pair : 2 * pair + 2, :, :],
                    flipped[u][pair][:].rearrange("p i half m -> p i m half"),
                )
            hop1_grouped[u] = grouped

        def quantise_hop1(u):
            codes = stage.tile([P, TILES * P], U32, name="hop1_codes%d" % u, tag="hop1_codes", align_bytes=64)
            scales = stage.tile([P, TILES * P], U8, name="hop1_scales%d" % u, tag="hop1_scales", align_bytes=64)
            nc.vector.quantize_mx(out=codes[:].bitcast(FP8X4), scales=scales[:], in_=hop1_grouped[u][:])
            hop1_codes[u] = codes
            hop1_scales[u] = scales

        def second_hop(u, engines):
            four_passes(u, hop1_codes[u], hop1_scales[u], hop2_out, "hop2_rows", engines)

        def regroup_x_bank(g, engine):
            regroup_x(g, 0, engine)
            regroup_x(g, 1, engine)

        for g in (0, 1, 2):
            transpose_x(g, flip_pool, "flip")
        transpose_x(3, acc_pool, "acc")
        for k in range(2):
            nc.tensor.matmul_mx(
                out=warm_out[:], lhsT=w_words[0][:, :P].bitcast(FP8X4), lhsT_scale=w_planes[0][:, :P],
                rhs=w_words[0][:].bitcast(FP8X4), rhs_scale=w_planes[0][:], start=True, stop=True,
            )
        for g in range(4):
            regroup_x_bank(g, "VS"[g % 2])
            if g % 2 == 1:
                transpose_x(4 + g // 2, flip_pool, "flip")
        quantise_x(0)
        quantise_x(1)
        regroup_x(4, 0, "S")
        first_hop(0, "VSVS")
        regroup_x(4, 1, "S")
        first_hop(1, "VSVS")
        round_on_gpsimd(0)
        transpose_x(6, flip_pool, "flip")
        regroup_x_bank(5, "S")
        first_hop(2, "VSVS")
        transpose_hop1(0)
        round_on_gpsimd(1)
        regroup_x_bank(6, "V")
        first_hop(3, "VSVS")
        transpose_x(7, flip_pool, "flip")
        regroup_hop1(0, "VS")
        transpose_hop1(1)
        regroup_x_bank(7, "S")
        quantise_hop1(0)
        round_hop1(2)
        regroup_hop1(1, "SS")
        quantise_x(2)
        second_hop(0, "SVSV")
        first_hop(4, "SVSV")
        transpose_x(8, flip_pool, "flip")
        transpose_hop1(2)
        quantise_hop1(1)
        for n in range(4, UNITS + HOP2_LAG):
            u_quant = n - QUANTISE_LAG
            u_hop2 = n - HOP2_LAG
            g_out = n + X_LEAD
            has_q = 0 <= u_quant < UNITS
            has_x = 4 <= g_out < X_BANKS
            has_h1 = BURST <= n < UNITS
            quants = [j for j in range(3, 8) if (2 * j - 1 if j % 2 == 0 else 2 * j - 2) * (j > 1) == n]
            products = (TILES if has_h1 else 0) + (TILES if 0 <= u_hop2 < UNITS else 0)
            copies = 2 * has_q + 2 * has_x + products
            has_r = 0 <= n - 1 < UNITS
            v_copies = max(0, (copies - has_q - len(quants) - 2 * has_r) // 2)
            small = 2 * has_q + 2 * has_x
            small_engines = "V" * min(small, v_copies) + "S" * max(0, small - v_copies)
            n_v = max(0, v_copies - small)
            engines = ["S"] * (products - n_v) + ["V"] * n_v
            if has_r:
                round_hop1(n - 1)
            if has_q:
                regroup_hop1(u_quant, small_engines[:2])
                small_engines = small_engines[2:]
            if has_x:
                regroup_x(g_out, 0, small_engines[0])
                regroup_x(g_out, 1, small_engines[1])
            if has_q:
                quantise_hop1(u_quant)
            for j in quants:
                quantise_x(j)
            if has_h1:
                first_hop(n, engines[:TILES])
                engines = engines[TILES:]
            if 0 <= u_hop2 < UNITS:
                four_passes(u_hop2, hop1_codes[u_hop2], hop1_scales[u_hop2], hop2_out, "hop2_rows", engines)
            if 0 <= n - TRANSPOSE_LAG < UNITS:
                transpose_hop1(n - TRANSPOSE_LAG)
            if n == 4:
                held = acc_pool.tile([P, NODES], F32, name="held_clock", tag="acc")
                for k in range(2):
                    nc.tensor.matmul(out=held[:], lhsT=warm[:, :P], rhs=warm[:], start=k == 0, stop=k == 1)
            if 4 <= g_out + 1 < X_BANKS:
                transpose_x(g_out + 1, flip_pool, "flip")
